import numpy as np
import ml_dtypes


def mxq(x, axis, fmt="e4m3"):
    dtype, down = {"e4m3": (ml_dtypes.float8_e4m3fn, 7), "e5m2": (ml_dtypes.float8_e5m2, 14)}[fmt]
    v = np.moveaxis(np.asarray(x, np.float32).astype(ml_dtypes.bfloat16).astype(np.float64), axis, -1)
    blocks = v.reshape(v.shape[:-1] + (-1, 32))
    amax = np.abs(blocks).max(-1, keepdims=True)
    byte = np.maximum(np.where(amax > 0, np.frexp(amax)[1] - 1 + 127, 0) - down, 1)
    scale = np.exp2(byte - 127.0)
    codes = (blocks / scale).astype(np.float32).astype(dtype).astype(np.float64)
    return np.moveaxis((codes * scale).reshape(v.shape), -1, axis)


WIDE = False


def mx_kscale(k):
    if not WIDE:
        return np.ones(k)
    levels = np.array([10, -10, 5, -5, 0])
    a = np.random.permutation(np.resize(levels, k // 512 * 4)).reshape(k // 512, 4)
    idx = np.arange(k)
    return np.exp2(a[idx // 512, idx % 128 // 32])


BF16 = ml_dtypes.bfloat16


def bf(x):
    return np.asarray(x, np.float32).astype(BF16)


def f64(x):
    return np.asarray(x).astype(np.float64)


B, DI, DH = 1024, 1024, 256


def sigmoid(v):
    return 1.0 / (1.0 + np.exp(-v))


def setup_inputs():
    s = mx_kscale(DI)
    n = np.random.standard_normal
    a, c = 0.7 / np.sqrt(DI), 0.7 / np.sqrt(DH)
    keep = np.random.uniform(size=B) < 0.9
    return {
        "x": bf(n((B, DI)) * s),
        "h_minors": bf(n((B, DH))),
        "c_minors": bf(n((B, DH))),
        "s0": bf(n((B, DH))),
        "s1": bf(n((B, DH))),
        "s2": bf(n((B, DH))),
        "mask": bf(keep * (0.5 + 0.5 * np.random.uniform(size=B))),
        "weight_ih": bf(n((7 * DH, DI)) * a / s),
        "bias_ih": bf(n(7 * DH) * 0.3),
        "weight_hh": bf(n((4 * DH, DH)) * c),
        "bias_hh": bf(n(4 * DH) * 0.3),
        "weight_sh0": bf(n((DH, DH)) * c),
        "bias_sh0": bf(n(DH) * 0.3),
        "weight_sh1": bf(n((DH, DH)) * c),
        "bias_sh1": bf(n(DH) * 0.3),
        "weight_sh2": bf(n((DH, DH)) * c),
        "bias_sh2": bf(n(DH) * 0.3),
    }


def reference(x, h_minors, c_minors, s0, s1, s2, mask, weight_ih, bias_ih, weight_hh, bias_hh,
              weight_sh0, bias_sh0, weight_sh1, bias_sh1, weight_sh2, bias_sh2):
    d = DH
    m = f64(mask)[:, None]

    tmp = (mxq(f64(x), 1, "e4m3") @ mxq(f64(weight_ih), 1, "e4m3").T) + f64(bias_ih)
    tmp2 = f64(h_minors) @ f64(weight_hh).T + f64(bias_hh)
    tmp3 = np.concatenate([
        f64(s0) @ f64(weight_sh0).T + f64(bias_sh0),
        f64(s1) @ f64(weight_sh1).T + f64(bias_sh1),
        f64(s2) @ f64(weight_sh2).T + f64(bias_sh2),
    ], axis=1)

    tmp_in, tmp_s = tmp[:, :4 * d], tmp[:, 4 * d:]
    pre = tmp_in + tmp2
    ifo = sigmoid(pre[:, :3 * d])
    c_hat = pre[:, 3 * d:]
    i_g, f_g, o_g = ifo[:, :d], ifo[:, d:2 * d], ifo[:, 2 * d:]

    c_t = (f_g * f64(c_minors) + i_g * np.tanh(c_hat)) * m
    tc = np.tanh(c_t) * m
    h = o_g * tc

    bg = sigmoid(tmp_s + tmp3)
    b0, b1, b2 = bg[:, :d], bg[:, d:2 * d], bg[:, 2 * d:]

    s_0 = (b0 + 1.0 - o_g) * tc
    s_1 = (b1 + 2.0 - o_g - s_0) * 0.5 * tc
    s_2 = (b2 + 3.0 - o_g - (2.0 * s_0 + s_1)) * (1.0 / 3.0) * tc

    return (h, c_t, s_0, s_1, s_2)

@@ -1,0 +1,403 @@
+from contextlib import ExitStack
+
+import concourse.mybir as mybir
+from concourse.masks import make_identity
+
+F32 = mybir.dt.float32
+BF16 = mybir.dt.bfloat16
+U32 = mybir.dt.uint32
+U8 = mybir.dt.uint8
+FP8X4 = mybir.dt.float8_e4m3fn_x4
+ACT = mybir.ActivationFunctionType
+ALU = mybir.AluOpType
+
+P = 128
+BATCH = 1024
+DI = 1024
+DH = 256
+GATES = 7 * DH
+ROW_TILES = BATCH // P
+GROUP = 2
+N_GROUPS = ROW_TILES // GROUP
+K_PASS = 4 * P
+PASSES = DI // K_PASS
+KT = DH // P
+BANK = 512
+CHUNKS = ((0, 512), (512, 512), (1024, 512), (1536, 256))
+PLAIN_GROUPS = ((0, 512, 0), (512, 512, 0), (1024, 256, 1), (1280, 256, 2), (1536, 256, 3))
+BIAS_IN_PSUM_FROM = 4 * DH
+PLAIN_ROW_TILES = GATES // P
+
+FLOPS = 2 * BATCH * (GATES * DI + 4 * DH * DH + 3 * DH * DH)
+
+
+def tile_share_lstm_cell_pa_kernel(
+    tc, x, h_minors, c_minors, s0, s1, s2, mask,
+    weight_ih, bias_ih, weight_hh, bias_hh,
+    weight_sh0, bias_sh0, weight_sh1, bias_sh1, weight_sh2, bias_sh2,
+    out_0, out_1, out_2, out_3, out_4,
+):
+    nc = tc.nc
+    with ExitStack() as ctx:
+        keep = ctx.enter_context(tc.tile_pool(name="keep", bufs=1))
+        stage = ctx.enter_context(tc.tile_pool(name="stage", bufs=2))
+        gate_pool = ctx.enter_context(tc.tile_pool(name="gate_pool", bufs=3))
+        work = ctx.enter_context(tc.tile_pool(name="work", bufs=2))
+        ps_t = ctx.enter_context(tc.psum_pool(name="ps_t", bufs=3))
+        ps_acc = ctx.enter_context(tc.psum_pool(name="ps_acc", bufs=5))
+
+        def by_row_tile(ap):
+            return ap.rearrange("(p r) d -> p r d", r=ROW_TILES)
+
+        x_view = by_row_tile(x)
+        act_views = [by_row_tile(a) for a in (h_minors, s0, s1, s2)]
+        out_views = [by_row_tile(o) for o in (out_0, out_1, out_2, out_3, out_4)]
+
+        x_sb = keep.tile([P, ROW_TILES, DI], BF16)
+        acts_sb = keep.tile([P, 4, ROW_TILES, DH], BF16)
+        c_sb = keep.tile([P, ROW_TILES, DH], BF16)
+        wih_sb = keep.tile([P, GATES // P, DI], BF16)
+        wplain_sb = keep.tile([P, PLAIN_ROW_TILES, DH], BF16)
+        wplain_t = keep.tile([P, KT, GATES], BF16)
+        bias_rows = keep.tile([P, GATES], BF16)
+        bias_bc = keep.tile([P, GATES], F32)
+        mask_bf = keep.tile([P, ROW_TILES], BF16)
+        mask_f = keep.tile([P, ROW_TILES], F32)
+        ident_bf = keep.tile([P, P], BF16)
+        ident_f = keep.tile([P, P], F32)
+        ones = keep.tile([P, P], BF16)
+        warm = keep.tile([P, 1], F32)
+        x_codes = keep.tile([P, ROW_TILES, PASSES, P], U32, align_bytes=64)
+        x_scales = keep.tile([P, ROW_TILES, PASSES, P], U8, align_bytes=64)
+        w_codes = [
+            keep.tile([P, PASSES, n], U32, align_bytes=64, name="w_codes%d" % j)
+            for j, (c0, n) in enumerate(CHUNKS)
+        ]
+        w_scales = [
+            keep.tile([P, PASSES, n], U8, align_bytes=64, name="w_scales%d" % j)
+            for j, (c0, n) in enumerate(CHUNKS)
+        ]
+
+        nc.vector.memset(warm[:], 0.0)
+        nc.vector.memset(bias_rows[:], 0.0)
+        nc.vector.memset(ones[:], 1.0)
+        make_identity(nc, ident_bf[:])
+
+        def as_row(vec):
+            return vec.rearrange("(o n) -> o n", o=1)
+
+        nc.scalar.dma_start(out=bias_rows[0:1, :], in_=as_row(bias_ih))
+        nc.scalar.dma_start(out=bias_rows[1:2, 0 : 4 * DH], in_=as_row(bias_hh))
+        for j, b in enumerate((bias_sh0, bias_sh1, bias_sh2)):
+            nc.gpsimd.dma_start(out=bias_rows[1:2, (4 + j) * DH : (5 + j) * DH], in_=as_row(b))
+        nc.gpsimd.dma_start(out=mask_bf[:], in_=mask.rearrange("(p r) -> p r", r=ROW_TILES))
+        make_identity(nc, ident_f[:])
+        nc.scalar.activation(out=warm[:], in_=warm[:], func=ACT.Sigmoid)
+
+        def load_weight_chunk(j):
+            c0, n = CHUNKS[j]
+            nc.sync.dma_start(
+                out=wih_sb[:, c0 // P : (c0 + n) // P, :],
+                in_=weight_ih[c0 : c0 + n, :].rearrange("(t p) k -> p t k", p=P),
+            )
+
+        def load_acts(rows):
+            for s in range(4):
+                nc.sync.dma_start(out=acts_sb[:, s, rows, :], in_=act_views[s][:, rows, :])
+
+        def load_x(q):
+            rows = slice(q * GROUP, (q + 1) * GROUP)
+            nc.sync.dma_start(out=x_sb[:, rows, :], in_=x_view[:, rows, :])
+
+        nc.sync.dma_start(
+            out=wplain_sb[:, 0:8, :], in_=weight_hh.rearrange("(t p) k -> p t k", p=P)
+        )
+        for j, w in enumerate((weight_sh0, weight_sh1, weight_sh2)):
+            nc.sync.dma_start(
+                out=wplain_sb[:, 8 + 2 * j : 10 + 2 * j, :],
+                in_=w.rearrange("(t p) k -> p t k", p=P),
+            )
+        load_acts(slice(0, GROUP))
+        load_x(0)
+        load_weight_chunk(0)
+        load_weight_chunk(1)
+        load_acts(slice(GROUP, 2 * GROUP))
+        load_weight_chunk(2)
+        load_weight_chunk(3)
+        load_x(1)
+        nc.sync.dma_start(out=c_sb[:], in_=by_row_tile(c_minors))
+        load_x(2)
+        load_acts(slice(2 * GROUP, ROW_TILES))
+        load_x(3)
+
+        def transpose_plain_weights():
+            for kt in range(KT):
+                for t0 in range(0, PLAIN_ROW_TILES, 8):
+                    count = min(8, PLAIN_ROW_TILES - t0)
+                    bank = ps_t.tile([P, 8, P], BF16, name="bank_w", tag="bank_t")
+                    for t in range(count):
+                        nc.tensor.transpose(
+                            bank[:, t, :], wplain_sb[:, t0 + t, kt * P : (kt + 1) * P], ident_bf[:]
+                        )
+                    nc.scalar.copy(
+                        out=wplain_t[:, kt, t0 * P : (t0 + count) * P],
+                        in_=bank[:, 0:count, :].rearrange("p t n -> p (t n)"),
+                    )
+
+        def broadcast_bias():
+            for c0, n in CHUNKS:
+                if c0 >= BIAS_IN_PSUM_FROM:
+                    continue
+                acc = ps_acc.tile([P, BANK], F32, name="acc_bias", tag="acc")
+                nc.tensor.matmul(
+                    acc[:, 0:n], lhsT=ones[:], rhs=bias_rows[:, c0 : c0 + n], start=True, stop=True
+                )
+                nc.vector.tensor_copy(out=bias_bc[:, c0 : c0 + n], in_=acc[:, 0:n])
+
+        def regroup(rows_bf16, grouped_words):
+            words = rows_bf16.bitcast(F32)
+            bank = ps_t.tile([P, 2 * PASSES, P], F32, name="bank_q", tag="bank_t")
+            for plane in range(2 * PASSES):
+                nc.tensor.transpose(
+                    bank[:, plane, :], words[:, plane * P : (plane + 1) * P], ident_f[:]
+                )
+            nc.scalar.copy(
+                out=grouped_words, in_=bank[:].rearrange("p (g u) n -> p g n u", u=2)
+            )
+
+        w_grouped_of = {}
+
+        def regroup_weight_chunk(j):
+            c0, n = CHUNKS[j]
+            grouped = stage.tile(
+                [P, PASSES, n, 4], BF16, align_bytes=64, name="w_grouped", tag="w_grouped"
+            )
+            w_grouped_of[j] = grouped
+            grouped_words = grouped[:].bitcast(F32)
+            for t in range(n // P):
+                regroup(wih_sb[:, c0 // P + t, :], grouped_words[:, :, t * P : (t + 1) * P, :])
+
+        def quantise_weight_chunk(j):
+            nc.vector.quantize_mx(
+                out=w_codes[j][:].rearrange("p g n -> p (g n)").bitcast(FP8X4),
+                scales=w_scales[j][:].rearrange("p g n -> p (g n)"),
+                in_=w_grouped_of[j][:].rearrange("p g n t -> p (g n t)"),
+            )
+
+        x_grouped_of = {}
+
+        def regroup_x(q):
+            grouped = stage.tile([P, GROUP, PASSES, P, 4], BF16, align_bytes=64, name="x_grouped")
+            x_grouped_of[q] = grouped
+            grouped_words = grouped[:].bitcast(F32)
+            for i in range(GROUP):
+                regroup(x_sb[:, q * GROUP + i, :], grouped_words[:, i, :, :, :])
+
+        def quantise_x(q):
+            rows = slice(q * GROUP, (q + 1) * GROUP)
+            nc.vector.quantize_mx(
+                out=x_codes[:, rows, :, :].rearrange("p r g b -> p (r g b)").bitcast(FP8X4),
+                scales=x_scales[:, rows, :, :].rearrange("p r g b -> p (r g b)"),
+                in_=x_grouped_of[q][:].rearrange("p r g b t -> p (r g b t)"),
+            )
+
+        acts_t_of = {}
+
+        def transpose_acts(q):
+            for i in range(GROUP):
+                r = q * GROUP + i
+                bank = ps_t.tile([P, 4, KT, P], BF16, name="bank_a", tag="bank_t")
+                for s in range(4):
+                    for kt in range(KT):
+                        nc.tensor.transpose(
+                            bank[:, s, kt, :], acts_sb[:, s, r, kt * P : (kt + 1) * P], ident_bf[:]
+                        )
+                acts_t = stage.tile([P, 4, KT, P], BF16, name="acts_t", bufs=2 * GROUP)
+                acts_t_of[r] = acts_t
+                nc.scalar.copy(out=acts_t[:], in_=bank[:])
+
+        gates_of = {}
+
+        def plain_rows(q, i):
+            if i == 0:
+                gates_of[q] = gate_pool.tile([P, GROUP, GATES], F32, name="gates")
+            gates = gates_of[q]
+            acts_t = acts_t_of[q * GROUP + i]
+            for c0, n in CHUNKS:
+                acc = ps_acc.tile([P, BANK], F32, name="acc_plain", tag="acc")
+                for g0, width, s in PLAIN_GROUPS:
+                    if c0 <= g0 < c0 + n:
+                        for kt in range(KT):
+                            nc.tensor.matmul(
+                                acc[:, g0 - c0 : g0 - c0 + width],
+                                lhsT=acts_t[:, s, kt, :],
+                                rhs=wplain_t[:, kt, g0 : g0 + width],
+                                start=(kt == 0),
+                                stop=(kt == KT - 1 and c0 < BIAS_IN_PSUM_FROM),
+                            )
+                        if c0 >= BIAS_IN_PSUM_FROM:
+                            nc.tensor.matmul(
+                                acc[:, g0 - c0 : g0 - c0 + width],
+                                lhsT=ones[:],
+                                rhs=bias_rows[:, g0 : g0 + width],
+                                start=False,
+                                stop=True,
+                            )
+                if c0 >= BIAS_IN_PSUM_FROM:
+                    nc.scalar.copy(out=gates[:, i, c0 : c0 + n], in_=acc[:, 0:n])
+                else:
+                    nc.vector.tensor_tensor(
+                        out=gates[:, i, c0 : c0 + n],
+                        in0=acc[:, 0:n],
+                        in1=bias_bc[:, c0 : c0 + n],
+                        op=ALU.add,
+                    )
+
+        def mx_chunk(q, i, j):
+            gates = gates_of[q]
+            r = q * GROUP + i
+            c0, n = CHUNKS[j]
+            acc = ps_acc.tile([P, BANK], F32, name="acc_mx", tag="acc")
+            for g in range(PASSES):
+                nc.tensor.matmul_mx(
+                    out=acc[:, 0:n],
+                    lhsT=x_codes[:, r, g, :].bitcast(FP8X4),
+                    lhsT_scale=x_scales[:, r, g, :],
+                    rhs=w_codes[j][:, g, :].bitcast(FP8X4),
+                    rhs_scale=w_scales[j][:, g, :],
+                    start=(g == 0),
+                    stop=(g == PASSES - 1),
+                )
+            nc.vector.tensor_tensor(
+                out=gates[:, i, c0 : c0 + n],
+                in0=acc[:, 0:n],
+                in1=gates[:, i, c0 : c0 + n],
+                op=ALU.add,
+            )
+
+        def mx_rows(q, i):
+            for j in range(len(CHUNKS)):
+                mx_chunk(q, i, j)
+
+        def squash_rows(q, i):
+            gates = gates_of[q]
+            for lo, hi, func in (
+                (0, 3 * DH, ACT.Sigmoid), (3 * DH, 4 * DH, ACT.Tanh), (4 * DH, 7 * DH, ACT.Sigmoid)
+            ):
+                nc.scalar.activation(out=gates[:, i, lo:hi], in_=gates[:, i, lo:hi], func=func)
+
+        cell_of = {}
+        outs_of = {}
+        t_cell_of = {}
+
+        def gate_views(q):
+            gates = gates_of[q]
+            i_g, f_g, o_g, c_hat = [gates[:, :, k * DH : (k + 1) * DH] for k in range(4)]
+            b_all = gates[:, :, 4 * DH : 7 * DH].rearrange("p i (j d) -> p i j d", j=3)
+            return i_g, f_g, o_g, c_hat, b_all
+
+        def combine_gates(q, engine):
+            i_g, f_g, o_g, c_hat, b_all = gate_views(q)
+            rows = slice(q * GROUP, (q + 1) * GROUP)
+            cell = work.tile([P, GROUP, DH], F32, name="cell")
+            fresh = work.tile([P, GROUP, DH], F32, name="fresh")
+            cell_of[q] = cell
+            engine.tensor_tensor(out=cell[:], in0=f_g, in1=c_sb[:, rows, :], op=ALU.mult)
+            engine.tensor_tensor(out=fresh[:], in0=i_g, in1=c_hat, op=ALU.mult)
+            engine.tensor_tensor(out=cell[:], in0=cell[:], in1=fresh[:], op=ALU.add)
+            engine.tensor_tensor(
+                out=b_all,
+                in0=b_all,
+                in1=o_g.unsqueeze(2).to_broadcast([P, GROUP, 3, DH]),
+                op=ALU.subtract,
+            )
+
+        def mask_cell(q):
+            cell = cell_of[q]
+            rows = slice(q * GROUP, (q + 1) * GROUP)
+            outs = work.tile([P, 5, GROUP, DH], F32, name="outs")
+            t_cell = work.tile([P, GROUP, DH], F32, name="t_cell")
+            outs_of[q] = outs
+            t_cell_of[q] = t_cell
+            row_mask = [mask_f[:, q * GROUP + i : q * GROUP + i + 1] for i in range(GROUP)]
+            for i in range(GROUP):
+                nc.scalar.activation(out=t_cell[:, i, :], in_=cell[:, i, :], func=ACT.Tanh, scale=row_mask[i])
+            for i in range(GROUP):
+                nc.scalar.activation(out=t_cell[:, i, :], in_=t_cell[:, i, :], func=ACT.Copy, scale=row_mask[i])
+            for i in range(GROUP):
+                nc.scalar.activation(out=outs[:, 1, i, :], in_=cell[:, i, :], func=ACT.Copy, scale=row_mask[i])
+            nc.sync.dma_start(out=out_views[1][:, rows, :], in_=outs[:, 1, :, :])
+
+        def hidden(q, engine):
+            i_g, f_g, o_g, c_hat, b_all = gate_views(q)
+            rows = slice(q * GROUP, (q + 1) * GROUP)
+            engine.tensor_tensor(out=outs_of[q][:, 0, :, :], in0=o_g, in1=t_cell_of[q][:], op=ALU.mult)
+            nc.sync.dma_start(out=out_views[0][:, rows, :], in_=outs_of[q][:, 0, :, :])
+
+        def finish(q):
+            i_g, f_g, o_g, c_hat, b_minus_o = gate_views(q)
+            rows = slice(q * GROUP, (q + 1) * GROUP)
+            outs = outs_of[q]
+            t_cell = t_cell_of[q]
+            h_out, c_out, s0_out, s1_out, s2_out = [outs[:, k, :, :] for k in range(5)]
+            e1 = work.tile([P, GROUP, DH], F32, name="e1")
+            e2 = work.tile([P, GROUP, DH], F32, name="e2")
+            stt = nc.vector.scalar_tensor_tensor
+            stt(out=s0_out, in0=b_minus_o[:, :, 0, :], scalar=1.0, in1=t_cell[:], op0=ALU.add, op1=ALU.mult)
+            nc.sync.dma_start(out=out_views[2][:, rows, :], in_=s0_out)
+            stt(out=e1[:], in0=b_minus_o[:, :, 1, :], scalar=2.0, in1=s0_out, op0=ALU.add, op1=ALU.subtract)
+            stt(out=e2[:], in0=s0_out, scalar=-2.0, in1=b_minus_o[:, :, 2, :], op0=ALU.mult, op1=ALU.add)
+            stt(out=s1_out, in0=e1[:], scalar=0.5, in1=t_cell[:], op0=ALU.mult, op1=ALU.mult)
+            nc.sync.dma_start(out=out_views[3][:, rows, :], in_=s1_out)
+            stt(out=e2[:], in0=e2[:], scalar=3.0, in1=s1_out, op0=ALU.add, op1=ALU.subtract)
+            stt(out=s2_out, in0=e2[:], scalar=1.0 / 3.0, in1=t_cell[:], op0=ALU.mult, op1=ALU.mult)
+            nc.sync.dma_start(out=out_views[4][:, rows, :], in_=s2_out)
+
+        def helper(q):
+            return nc.vector if q == N_GROUPS - 1 else nc.gpsimd
+
+        transpose_plain_weights()
+        broadcast_bias()
+        transpose_acts(0)
+        plain_rows(0, 0)
+        regroup_x(0)
+        plain_rows(0, 1)
+        regroup_weight_chunk(0)
+        transpose_acts(1)
+        quantise_x(0)
+        for j in range(len(CHUNKS)):
+            quantise_weight_chunk(j)
+            if j < GROUP:
+                plain_rows(1, j)
+            if j + 1 < len(CHUNKS):
+                regroup_weight_chunk(j + 1)
+            mx_chunk(0, 0, j)
+            mx_chunk(0, 1, j)
+        transpose_acts(2)
+        regroup_x(1)
+        squash_rows(0, 0)
+        regroup_x(2)
+        squash_rows(0, 1)
+        nc.vector.tensor_copy(out=mask_f[:], in_=mask_bf[:])
+        combine_gates(0, helper(0))
+        quantise_x(1)
+        for q in range(N_GROUPS):
+            if q + 2 < N_GROUPS:
+                plain_rows(q + 2, 0)
+                plain_rows(q + 2, 1)
+            mask_cell(q)
+            hidden(q, helper(q))
+            if q + 1 < N_GROUPS:
+                mx_rows(q + 1, 0)
+                squash_rows(q + 1, 0)
+                mx_rows(q + 1, 1)
+            if q + 3 < N_GROUPS:
+                transpose_acts(q + 3)
+                regroup_x(q + 3)
+            if q + 1 < N_GROUPS:
+                squash_rows(q + 1, 1)
+            if q + 2 < N_GROUPS:
+                quantise_x(q + 2)
+            finish(q)
+            if q + 1 < N_GROUPS:
+                combine_gates(q + 1, helper(q + 1))

@@ -17,8 +17,6 @@ DI = 1024
 DH = 256
 GATES = 7 * DH
 ROW_TILES = BATCH // P
-GROUP = 2
-N_GROUPS = ROW_TILES // GROUP
 K_PASS = 4 * P
 PASSES = DI // K_PASS
 KT = DH // P
@@ -27,6 +25,12 @@ CHUNKS = ((0, 512), (512, 512), (1024, 512), (1536, 256))
 PLAIN_GROUPS = ((0, 512, 0), (512, 512, 0), (1024, 256, 1), (1280, 256, 2), (1536, 256, 3))
 BIAS_IN_PSUM_FROM = 4 * DH
 PLAIN_ROW_TILES = GATES // P
+CORE = (0, 1)
+SHARED = (2, 3)
+SHARED_AHEAD = 1
+CORE_AHEAD = 2
+PLAIN_AHEAD = 3
+PREP_AHEAD = 5
 
 FLOPS = 2 * BATCH * (GATES * DI + 4 * DH * DH + 3 * DH * DH)
 
@@ -41,10 +45,11 @@ def tile_share_lstm_cell_pa_kernel(
     with ExitStack() as ctx:
         keep = ctx.enter_context(tc.tile_pool(name="keep", bufs=1))
         stage = ctx.enter_context(tc.tile_pool(name="stage", bufs=2))
-        gate_pool = ctx.enter_context(tc.tile_pool(name="gate_pool", bufs=3))
-        work = ctx.enter_context(tc.tile_pool(name="work", bufs=2))
+        gate_pool = ctx.enter_context(tc.tile_pool(name="gate_pool", bufs=PLAIN_AHEAD + 2))
+        work = ctx.enter_context(tc.tile_pool(name="work", bufs=CORE_AHEAD + 2))
         ps_t = ctx.enter_context(tc.psum_pool(name="ps_t", bufs=3))
         ps_acc = ctx.enter_context(tc.psum_pool(name="ps_acc", bufs=5))
+        ctx.enter_context(tc.manual_schedule())
 
         def by_row_tile(ap):
             return ap.rearrange("(p r) d -> p r d", r=ROW_TILES)
@@ -60,7 +65,7 @@ def tile_share_lstm_cell_pa_kernel(
         wplain_sb = keep.tile([P, PLAIN_ROW_TILES, DH], BF16)
         wplain_t = keep.tile([P, KT, GATES], BF16)
         bias_rows = keep.tile([P, GATES], BF16)
-        bias_bc = keep.tile([P, GATES], F32)
+        bias_bc = keep.tile([P, BIAS_IN_PSUM_FROM], F32)
         mask_bf = keep.tile([P, ROW_TILES], BF16)
         mask_f = keep.tile([P, ROW_TILES], F32)
         ident_bf = keep.tile([P, P], BF16)
@@ -101,12 +106,10 @@ def tile_share_lstm_cell_pa_kernel(
                 in_=weight_ih[c0 : c0 + n, :].rearrange("(t p) k -> p t k", p=P),
             )
 
-        def load_acts(rows):
+        def load_rows(first, count):
+            rows = slice(first, first + count)
             for s in range(4):
                 nc.sync.dma_start(out=acts_sb[:, s, rows, :], in_=act_views[s][:, rows, :])
-
-        def load_x(q):
-            rows = slice(q * GROUP, (q + 1) * GROUP)
             nc.sync.dma_start(out=x_sb[:, rows, :], in_=x_view[:, rows, :])
 
         nc.sync.dma_start(
@@ -117,53 +120,55 @@ def tile_share_lstm_cell_pa_kernel(
                 out=wplain_sb[:, 8 + 2 * j : 10 + 2 * j, :],
                 in_=w.rearrange("(t p) k -> p t k", p=P),
             )
-        load_acts(slice(0, GROUP))
-        load_x(0)
+        load_rows(0, 2)
         load_weight_chunk(0)
         load_weight_chunk(1)
-        load_acts(slice(GROUP, 2 * GROUP))
+        nc.sync.dma_start(out=c_sb[:], in_=by_row_tile(c_minors))
         load_weight_chunk(2)
         load_weight_chunk(3)
-        load_x(1)
-        nc.sync.dma_start(out=c_sb[:], in_=by_row_tile(c_minors))
-        load_x(2)
-        load_acts(slice(2 * GROUP, ROW_TILES))
-        load_x(3)
+        load_rows(2, 2)
+        load_rows(4, 4)
+
+        def copy_out(turn, out, in_):
+            if turn % 2 == 0:
+                nc.scalar.copy(out=out, in_=in_)
+            else:
+                nc.vector.tensor_copy(out=out, in_=in_)
 
         def transpose_plain_weights():
-            for kt in range(KT):
-                for t0 in range(0, PLAIN_ROW_TILES, 8):
-                    count = min(8, PLAIN_ROW_TILES - t0)
+            turn = 0
+            for t0 in range(0, PLAIN_ROW_TILES, 8):
+                count = min(8, PLAIN_ROW_TILES - t0)
+                for kt in range(KT):
                     bank = ps_t.tile([P, 8, P], BF16, name="bank_w", tag="bank_t")
                     for t in range(count):
                         nc.tensor.transpose(
                             bank[:, t, :], wplain_sb[:, t0 + t, kt * P : (kt + 1) * P], ident_bf[:]
                         )
-                    nc.scalar.copy(
-                        out=wplain_t[:, kt, t0 * P : (t0 + count) * P],
-                        in_=bank[:, 0:count, :].rearrange("p t n -> p (t n)"),
+                    copy_out(
+                        turn,
+                        wplain_t[:, kt, t0 * P : (t0 + count) * P],
+                        bank[:, 0:count, :].rearrange("p t n -> p (t n)"),
                     )
+                    turn += 1
 
         def broadcast_bias():
             for c0, n in CHUNKS:
-                if c0 >= BIAS_IN_PSUM_FROM:
-                    continue
-                acc = ps_acc.tile([P, BANK], F32, name="acc_bias", tag="acc")
-                nc.tensor.matmul(
-                    acc[:, 0:n], lhsT=ones[:], rhs=bias_rows[:, c0 : c0 + n], start=True, stop=True
-                )
-                nc.vector.tensor_copy(out=bias_bc[:, c0 : c0 + n], in_=acc[:, 0:n])
+                if c0 < BIAS_IN_PSUM_FROM:
+                    acc = ps_acc.tile([P, BANK], F32, name="acc_bias", tag="acc")
+                    nc.tensor.matmul(
+                        acc[:, 0:n], lhsT=ones[:], rhs=bias_rows[:, c0 : c0 + n], start=True, stop=True
+                    )
+                    nc.vector.tensor_copy(out=bias_bc[:, c0 : c0 + n], in_=acc[:, 0:n])
 
-        def regroup(rows_bf16, grouped_words):
+        def regroup(turn, rows_bf16, grouped_words):
             words = rows_bf16.bitcast(F32)
             bank = ps_t.tile([P, 2 * PASSES, P], F32, name="bank_q", tag="bank_t")
             for plane in range(2 * PASSES):
                 nc.tensor.transpose(
                     bank[:, plane, :], words[:, plane * P : (plane + 1) * P], ident_f[:]
                 )
-            nc.scalar.copy(
-                out=grouped_words, in_=bank[:].rearrange("p (g u) n -> p g n u", u=2)
-            )
+            copy_out(turn, grouped_words, bank[:].rearrange("p (g u) n -> p g n u", u=2))
 
         w_grouped_of = {}
 
@@ -175,7 +180,7 @@ def tile_share_lstm_cell_pa_kernel(
             w_grouped_of[j] = grouped
             grouped_words = grouped[:].bitcast(F32)
             for t in range(n // P):
-                regroup(wih_sb[:, c0 // P + t, :], grouped_words[:, :, t * P : (t + 1) * P, :])
+                regroup(t, wih_sb[:, c0 // P + t, :], grouped_words[:, :, t * P : (t + 1) * P, :])
 
         def quantise_weight_chunk(j):
             nc.vector.quantize_mx(
@@ -185,219 +190,196 @@ def tile_share_lstm_cell_pa_kernel(
             )
 
         x_grouped_of = {}
-
-        def regroup_x(q):
-            grouped = stage.tile([P, GROUP, PASSES, P, 4], BF16, align_bytes=64, name="x_grouped")
-            x_grouped_of[q] = grouped
-            grouped_words = grouped[:].bitcast(F32)
-            for i in range(GROUP):
-                regroup(x_sb[:, q * GROUP + i, :], grouped_words[:, i, :, :, :])
-
-        def quantise_x(q):
-            rows = slice(q * GROUP, (q + 1) * GROUP)
-            nc.vector.quantize_mx(
-                out=x_codes[:, rows, :, :].rearrange("p r g b -> p (r g b)").bitcast(FP8X4),
-                scales=x_scales[:, rows, :, :].rearrange("p r g b -> p (r g b)"),
-                in_=x_grouped_of[q][:].rearrange("p r g b t -> p (r g b t)"),
-            )
-
         acts_t_of = {}
 
-        def transpose_acts(q):
-            for i in range(GROUP):
-                r = q * GROUP + i
-                bank = ps_t.tile([P, 4, KT, P], BF16, name="bank_a", tag="bank_t")
-                for s in range(4):
-                    for kt in range(KT):
-                        nc.tensor.transpose(
-                            bank[:, s, kt, :], acts_sb[:, s, r, kt * P : (kt + 1) * P], ident_bf[:]
-                        )
-                acts_t = stage.tile([P, 4, KT, P], BF16, name="acts_t", bufs=2 * GROUP)
-                acts_t_of[r] = acts_t
-                nc.scalar.copy(out=acts_t[:], in_=bank[:])
+        def prepare_rows(r):
+            bank = ps_t.tile([P, 4, KT, P], BF16, name="bank_a", tag="bank_t")
+            for s in range(4):
+                for kt in range(KT):
+                    nc.tensor.transpose(
+                        bank[:, s, kt, :], acts_sb[:, s, r, kt * P : (kt + 1) * P], ident_bf[:]
+                    )
+            acts_t_of[r] = stage.tile([P, 4, KT, P], BF16, name="acts_t", bufs=PREP_AHEAD + 1)
+            nc.scalar.copy(out=acts_t_of[r][:], in_=bank[:])
+            x_grouped_of[r] = stage.tile(
+                [P, PASSES, P, 4], BF16, align_bytes=64, name="x_grouped", bufs=PREP_AHEAD
+            )
+            regroup(0, x_sb[:, r, :], x_grouped_of[r][:].bitcast(F32))
+
+        def quantise_x(r):
+            nc.vector.quantize_mx(
+                out=x_codes[:, r, :, :].rearrange("p g b -> p (g b)").bitcast(FP8X4),
+                scales=x_scales[:, r, :, :].rearrange("p g b -> p (g b)"),
+                in_=x_grouped_of[r][:].rearrange("p g b t -> p (g b t)"),
+            )
 
         gates_of = {}
 
-        def plain_rows(q, i):
-            if i == 0:
-                gates_of[q] = gate_pool.tile([P, GROUP, GATES], F32, name="gates")
-            gates = gates_of[q]
-            acts_t = acts_t_of[q * GROUP + i]
+        def plain_rows(r):
+            gates = gate_pool.tile([P, GATES], F32, name="gates")
+            gates_of[r] = gates
+            acts_t = acts_t_of[r]
             for c0, n in CHUNKS:
+                bias_in_psum = c0 >= BIAS_IN_PSUM_FROM
                 acc = ps_acc.tile([P, BANK], F32, name="acc_plain", tag="acc")
                 for g0, width, s in PLAIN_GROUPS:
                     if c0 <= g0 < c0 + n:
+                        cols = acc[:, g0 - c0 : g0 - c0 + width]
                         for kt in range(KT):
                             nc.tensor.matmul(
-                                acc[:, g0 - c0 : g0 - c0 + width],
+                                cols,
                                 lhsT=acts_t[:, s, kt, :],
                                 rhs=wplain_t[:, kt, g0 : g0 + width],
                                 start=(kt == 0),
-                                stop=(kt == KT - 1 and c0 < BIAS_IN_PSUM_FROM),
+                                stop=(kt == KT - 1 and not bias_in_psum),
                             )
-                        if c0 >= BIAS_IN_PSUM_FROM:
+                        if bias_in_psum:
                             nc.tensor.matmul(
-                                acc[:, g0 - c0 : g0 - c0 + width],
-                                lhsT=ones[:],
-                                rhs=bias_rows[:, g0 : g0 + width],
-                                start=False,
-                                stop=True,
+                                cols, lhsT=ones[:], rhs=bias_rows[:, g0 : g0 + width], start=False, stop=True
                             )
-                if c0 >= BIAS_IN_PSUM_FROM:
-                    nc.scalar.copy(out=gates[:, i, c0 : c0 + n], in_=acc[:, 0:n])
+                if bias_in_psum:
+                    nc.scalar.copy(out=gates[:, c0 : c0 + n], in_=acc[:, 0:n])
                 else:
                     nc.vector.tensor_tensor(
-                        out=gates[:, i, c0 : c0 + n],
-                        in0=acc[:, 0:n],
-                        in1=bias_bc[:, c0 : c0 + n],
-                        op=ALU.add,
+                        out=gates[:, c0 : c0 + n], in0=acc[:, 0:n], in1=bias_bc[:, c0 : c0 + n], op=ALU.add
                     )
 
-        def mx_chunk(q, i, j):
-            gates = gates_of[q]
-            r = q * GROUP + i
-            c0, n = CHUNKS[j]
-            acc = ps_acc.tile([P, BANK], F32, name="acc_mx", tag="acc")
-            for g in range(PASSES):
-                nc.tensor.matmul_mx(
-                    out=acc[:, 0:n],
-                    lhsT=x_codes[:, r, g, :].bitcast(FP8X4),
-                    lhsT_scale=x_scales[:, r, g, :],
-                    rhs=w_codes[j][:, g, :].bitcast(FP8X4),
-                    rhs_scale=w_scales[j][:, g, :],
-                    start=(g == 0),
-                    stop=(g == PASSES - 1),
+        def mx_rows(r, chunk_ids):
+            gates = gates_of[r]
+            for j in chunk_ids:
+                c0, n = CHUNKS[j]
+                acc = ps_acc.tile([P, BANK], F32, name="acc_mx", tag="acc")
+                for g in range(PASSES):
+                    nc.tensor.matmul_mx(
+                        out=acc[:, 0:n],
+                        lhsT=x_codes[:, r, g, :].bitcast(FP8X4),
+                        lhsT_scale=x_scales[:, r, g, :],
+                        rhs=w_codes[j][:, g, :].bitcast(FP8X4),
+                        rhs_scale=w_scales[j][:, g, :],
+                        start=(g == 0),
+                        stop=(g == PASSES - 1),
+                    )
+                nc.vector.tensor_tensor(
+                    out=gates[:, c0 : c0 + n], in0=acc[:, 0:n], in1=gates[:, c0 : c0 + n], op=ALU.add
                 )
-            nc.vector.tensor_tensor(
-                out=gates[:, i, c0 : c0 + n],
-                in0=acc[:, 0:n],
-                in1=gates[:, i, c0 : c0 + n],
-                op=ALU.add,
-            )
 
-        def mx_rows(q, i):
-            for j in range(len(CHUNKS)):
-                mx_chunk(q, i, j)
+        def squash(r, lo, hi, func):
+            gates = gates_of[r]
+            nc.scalar.activation(out=gates[:, lo:hi], in_=gates[:, lo:hi], func=func)
 
-        def squash_rows(q, i):
-            gates = gates_of[q]
-            for lo, hi, func in (
-                (0, 3 * DH, ACT.Sigmoid), (3 * DH, 4 * DH, ACT.Tanh), (4 * DH, 7 * DH, ACT.Sigmoid)
-            ):
-                nc.scalar.activation(out=gates[:, i, lo:hi], in_=gates[:, i, lo:hi], func=func)
+        def squash_core(r):
+            squash(r, 0, 3 * DH, ACT.Sigmoid)
+            squash(r, 3 * DH, 4 * DH, ACT.Tanh)
+
+        def squash_shared(r):
+            squash(r, 4 * DH, 7 * DH, ACT.Sigmoid)
 
         cell_of = {}
         outs_of = {}
         t_cell_of = {}
 
-        def gate_views(q):
-            gates = gates_of[q]
-            i_g, f_g, o_g, c_hat = [gates[:, :, k * DH : (k + 1) * DH] for k in range(4)]
-            b_all = gates[:, :, 4 * DH : 7 * DH].rearrange("p i (j d) -> p i j d", j=3)
+        def gate_views(r):
+            gates = gates_of[r]
+            i_g, f_g, o_g, c_hat = [gates[:, k * DH : (k + 1) * DH] for k in range(4)]
+            b_all = gates[:, 4 * DH : 7 * DH].rearrange("p (j d) -> p j d", j=3)
             return i_g, f_g, o_g, c_hat, b_all
 
-        def combine_gates(q, engine):
-            i_g, f_g, o_g, c_hat, b_all = gate_views(q)
-            rows = slice(q * GROUP, (q + 1) * GROUP)
-            cell = work.tile([P, GROUP, DH], F32, name="cell")
-            fresh = work.tile([P, GROUP, DH], F32, name="fresh")
-            cell_of[q] = cell
-            engine.tensor_tensor(out=cell[:], in0=f_g, in1=c_sb[:, rows, :], op=ALU.mult)
+        def combine_core(r, engine):
+            i_g, f_g, o_g, c_hat, b_all = gate_views(r)
+            cell = work.tile([P, DH], F32, name="cell")
+            fresh = work.tile([P, DH], F32, name="fresh")
+            cell_of[r] = cell
+            engine.tensor_tensor(out=cell[:], in0=f_g, in1=c_sb[:, r, :], op=ALU.mult)
             engine.tensor_tensor(out=fresh[:], in0=i_g, in1=c_hat, op=ALU.mult)
             engine.tensor_tensor(out=cell[:], in0=cell[:], in1=fresh[:], op=ALU.add)
+
+        def combine_shared(r, engine):
+            i_g, f_g, o_g, c_hat, b_all = gate_views(r)
             engine.tensor_tensor(
-                out=b_all,
-                in0=b_all,
-                in1=o_g.unsqueeze(2).to_broadcast([P, GROUP, 3, DH]),
-                op=ALU.subtract,
+                out=b_all, in0=b_all, in1=o_g.unsqueeze(1).to_broadcast([P, 3, DH]), op=ALU.subtract
             )
 
-        def mask_cell(q):
-            cell = cell_of[q]
-            rows = slice(q * GROUP, (q + 1) * GROUP)
-            outs = work.tile([P, 5, GROUP, DH], F32, name="outs")
-            t_cell = work.tile([P, GROUP, DH], F32, name="t_cell")
-            outs_of[q] = outs
-            t_cell_of[q] = t_cell
-            row_mask = [mask_f[:, q * GROUP + i : q * GROUP + i + 1] for i in range(GROUP)]
-            for i in range(GROUP):
-                nc.scalar.activation(out=t_cell[:, i, :], in_=cell[:, i, :], func=ACT.Tanh, scale=row_mask[i])
-            for i in range(GROUP):
-                nc.scalar.activation(out=t_cell[:, i, :], in_=t_cell[:, i, :], func=ACT.Copy, scale=row_mask[i])
-            for i in range(GROUP):
-                nc.scalar.activation(out=outs[:, 1, i, :], in_=cell[:, i, :], func=ACT.Copy, scale=row_mask[i])
-            nc.sync.dma_start(out=out_views[1][:, rows, :], in_=outs[:, 1, :, :])
+        def mask_cell(r):
+            cell = cell_of[r]
+            outs = work.tile([P, 5, DH], F32, name="outs")
+            t_cell = work.tile([P, DH], F32, name="t_cell")
+            outs_of[r] = outs
+            t_cell_of[r] = t_cell
+            m = mask_f[:, r : r + 1]
+            nc.scalar.activation(out=t_cell[:], in_=cell[:], func=ACT.Tanh, scale=m)
+            nc.scalar.activation(out=t_cell[:], in_=t_cell[:], func=ACT.Copy, scale=m)
+            nc.scalar.activation(out=outs[:, 1, :], in_=cell[:], func=ACT.Copy, scale=m)
+            nc.sync.dma_start(out=out_views[1][:, r, :], in_=outs[:, 1, :])
 
-        def hidden(q, engine):
-            i_g, f_g, o_g, c_hat, b_all = gate_views(q)
-            rows = slice(q * GROUP, (q + 1) * GROUP)
-            engine.tensor_tensor(out=outs_of[q][:, 0, :, :], in0=o_g, in1=t_cell_of[q][:], op=ALU.mult)
-            nc.sync.dma_start(out=out_views[0][:, rows, :], in_=outs_of[q][:, 0, :, :])
-
-        def finish(q):
-            i_g, f_g, o_g, c_hat, b_minus_o = gate_views(q)
-            rows = slice(q * GROUP, (q + 1) * GROUP)
-            outs = outs_of[q]
-            t_cell = t_cell_of[q]
-            h_out, c_out, s0_out, s1_out, s2_out = [outs[:, k, :, :] for k in range(5)]
-            e1 = work.tile([P, GROUP, DH], F32, name="e1")
-            e2 = work.tile([P, GROUP, DH], F32, name="e2")
+        def finish(r):
+            i_g, f_g, o_g, c_hat, b_minus_o = gate_views(r)
+            outs = outs_of[r]
+            t_cell = t_cell_of[r]
+            h_out, c_out, s0_out, s1_out, s2_out = [outs[:, k, :] for k in range(5)]
+            e1 = work.tile([P, DH], F32, name="e1")
+            e2 = work.tile([P, DH], F32, name="e2")
             stt = nc.vector.scalar_tensor_tensor
-            stt(out=s0_out, in0=b_minus_o[:, :, 0, :], scalar=1.0, in1=t_cell[:], op0=ALU.add, op1=ALU.mult)
-            nc.sync.dma_start(out=out_views[2][:, rows, :], in_=s0_out)
-            stt(out=e1[:], in0=b_minus_o[:, :, 1, :], scalar=2.0, in1=s0_out, op0=ALU.add, op1=ALU.subtract)
-            stt(out=e2[:], in0=s0_out, scalar=-2.0, in1=b_minus_o[:, :, 2, :], op0=ALU.mult, op1=ALU.add)
+            stt(out=s0_out, in0=b_minus_o[:, 0, :], scalar=1.0, in1=t_cell[:], op0=ALU.add, op1=ALU.mult)
+            nc.vector.tensor_tensor(out=h_out, in0=o_g, in1=t_cell[:], op=ALU.mult)
+            stt(out=e1[:], in0=b_minus_o[:, 1, :], scalar=2.0, in1=s0_out, op0=ALU.add, op1=ALU.subtract)
+            stt(out=e2[:], in0=s0_out, scalar=-2.0, in1=b_minus_o[:, 2, :], op0=ALU.mult, op1=ALU.add)
             stt(out=s1_out, in0=e1[:], scalar=0.5, in1=t_cell[:], op0=ALU.mult, op1=ALU.mult)
-            nc.sync.dma_start(out=out_views[3][:, rows, :], in_=s1_out)
             stt(out=e2[:], in0=e2[:], scalar=3.0, in1=s1_out, op0=ALU.add, op1=ALU.subtract)
             stt(out=s2_out, in0=e2[:], scalar=1.0 / 3.0, in1=t_cell[:], op0=ALU.mult, op1=ALU.mult)
-            nc.sync.dma_start(out=out_views[4][:, rows, :], in_=s2_out)
+            for k in (0, 2, 3, 4):
+                nc.sync.dma_start(out=out_views[k][:, r, :], in_=outs[:, k, :])
 
-        def helper(q):
-            return nc.vector if q == N_GROUPS - 1 else nc.gpsimd
+        def helper(r):
+            return nc.vector if r >= ROW_TILES - 1 else nc.gpsimd
+
+        def core(r):
+            mx_rows(r, CORE)
+            squash_core(r)
 
         transpose_plain_weights()
         broadcast_bias()
-        transpose_acts(0)
-        plain_rows(0, 0)
-        regroup_x(0)
-        plain_rows(0, 1)
-        regroup_weight_chunk(0)
-        transpose_acts(1)
+        prepare_rows(0)
+        prepare_rows(1)
+        plain_rows(0)
         quantise_x(0)
-        for j in range(len(CHUNKS)):
-            quantise_weight_chunk(j)
-            if j < GROUP:
-                plain_rows(1, j)
-            if j + 1 < len(CHUNKS):
-                regroup_weight_chunk(j + 1)
-            mx_chunk(0, 0, j)
-            mx_chunk(0, 1, j)
-        transpose_acts(2)
-        regroup_x(1)
-        squash_rows(0, 0)
-        regroup_x(2)
-        squash_rows(0, 1)
-        nc.vector.tensor_copy(out=mask_f[:], in_=mask_bf[:])
-        combine_gates(0, helper(0))
+        regroup_weight_chunk(0)
         quantise_x(1)
-        for q in range(N_GROUPS):
-            if q + 2 < N_GROUPS:
-                plain_rows(q + 2, 0)
-                plain_rows(q + 2, 1)
-            mask_cell(q)
-            hidden(q, helper(q))
-            if q + 1 < N_GROUPS:
-                mx_rows(q + 1, 0)
-                squash_rows(q + 1, 0)
-                mx_rows(q + 1, 1)
-            if q + 3 < N_GROUPS:
-                transpose_acts(q + 3)
-                regroup_x(q + 3)
-            if q + 1 < N_GROUPS:
-                squash_rows(q + 1, 1)
-            if q + 2 < N_GROUPS:
-                quantise_x(q + 2)
-            finish(q)
-            if q + 1 < N_GROUPS:
-                combine_gates(q + 1, helper(q + 1))
+        plain_rows(1)
+        regroup_weight_chunk(1)
+        quantise_weight_chunk(0)
+        quantise_weight_chunk(1)
+        regroup_weight_chunk(2)
+        mx_rows(0, CORE)
+        mx_rows(1, CORE)
+        regroup_weight_chunk(3)
+        squash_core(0)
+        combine_core(0, helper(0))
+        squash_core(1)
+        combine_core(1, helper(1))
+        quantise_weight_chunk(2)
+        quantise_weight_chunk(3)
+        nc.vector.tensor_copy(out=mask_f[:], in_=mask_bf[:])
+        prepare_rows(2)
+        prepare_rows(3)
+        plain_rows(2)
+        prepare_rows(4)
+        quantise_x(2)
+        for n in range(-SHARED_AHEAD, ROW_TILES):
+            if n + SHARED_AHEAD < ROW_TILES:
+                mx_rows(n + SHARED_AHEAD, SHARED)
+                squash_shared(n + SHARED_AHEAD)
+                mask_cell(n + SHARED_AHEAD)
+            if PLAIN_AHEAD <= n + PLAIN_AHEAD < ROW_TILES:
+                plain_rows(n + PLAIN_AHEAD)
+            if CORE_AHEAD <= n + CORE_AHEAD < ROW_TILES:
+                core(n + CORE_AHEAD)
+            if PREP_AHEAD <= n + PREP_AHEAD < ROW_TILES:
+                prepare_rows(n + PREP_AHEAD)
+            if n + SHARED_AHEAD < ROW_TILES:
+                combine_shared(n + SHARED_AHEAD, helper(n + PLAIN_AHEAD))
+            if PLAIN_AHEAD <= n + PLAIN_AHEAD < ROW_TILES:
+                quantise_x(n + PLAIN_AHEAD)
+            if n >= 0:
+                finish(n)
+            if CORE_AHEAD <= n + CORE_AHEAD < ROW_TILES:
+                combine_core(n + CORE_AHEAD, helper(n + CORE_AHEAD))

@@ -27,10 +27,8 @@ BIAS_IN_PSUM_FROM = 4 * DH
 PLAIN_ROW_TILES = GATES // P
 CORE = (0, 1)
 SHARED = (2, 3)
-SHARED_AHEAD = 1
-CORE_AHEAD = 2
-PLAIN_AHEAD = 3
-PREP_AHEAD = 5
+PAIR = 2
+N_PAIRS = ROW_TILES // PAIR
 
 FLOPS = 2 * BATCH * (GATES * DI + 4 * DH * DH + 3 * DH * DH)
 
@@ -45,10 +43,9 @@ def tile_share_lstm_cell_pa_kernel(
     with ExitStack() as ctx:
         keep = ctx.enter_context(tc.tile_pool(name="keep", bufs=1))
         stage = ctx.enter_context(tc.tile_pool(name="stage", bufs=2))
-        gate_pool = ctx.enter_context(tc.tile_pool(name="gate_pool", bufs=PLAIN_AHEAD + 2))
-        work = ctx.enter_context(tc.tile_pool(name="work", bufs=CORE_AHEAD + 2))
-        ps_t = ctx.enter_context(tc.psum_pool(name="ps_t", bufs=3))
-        ps_acc = ctx.enter_context(tc.psum_pool(name="ps_acc", bufs=5))
+        gate_pool = ctx.enter_context(tc.tile_pool(name="gate_pool", bufs=3))
+        work = ctx.enter_context(tc.tile_pool(name="work", bufs=2))
+        psum = ctx.enter_context(tc.psum_pool(name="psum", bufs=8))
         ctx.enter_context(tc.manual_schedule())
 
         def by_row_tile(ap):
@@ -140,7 +137,7 @@ def tile_share_lstm_cell_pa_kernel(
             for t0 in range(0, PLAIN_ROW_TILES, 8):
                 count = min(8, PLAIN_ROW_TILES - t0)
                 for kt in range(KT):
-                    bank = ps_t.tile([P, 8, P], BF16, name="bank_w", tag="bank_t")
+                    bank = psum.tile([P, 8, P], BF16, name="bank_w", tag="bank")
                     for t in range(count):
                         nc.tensor.transpose(
                             bank[:, t, :], wplain_sb[:, t0 + t, kt * P : (kt + 1) * P], ident_bf[:]
@@ -155,7 +152,7 @@ def tile_share_lstm_cell_pa_kernel(
         def broadcast_bias():
             for c0, n in CHUNKS:
                 if c0 < BIAS_IN_PSUM_FROM:
-                    acc = ps_acc.tile([P, BANK], F32, name="acc_bias", tag="acc")
+                    acc = psum.tile([P, BANK], F32, name="acc_bias", tag="bank")
                     nc.tensor.matmul(
                         acc[:, 0:n], lhsT=ones[:], rhs=bias_rows[:, c0 : c0 + n], start=True, stop=True
                     )
@@ -163,7 +160,7 @@ def tile_share_lstm_cell_pa_kernel(
 
         def regroup(turn, rows_bf16, grouped_words):
             words = rows_bf16.bitcast(F32)
-            bank = ps_t.tile([P, 2 * PASSES, P], F32, name="bank_q", tag="bank_t")
+            bank = psum.tile([P, 2 * PASSES, P], F32, name="bank_q", tag="bank")
             for plane in range(2 * PASSES):
                 nc.tensor.transpose(
                     bank[:, plane, :], words[:, plane * P : (plane + 1) * P], ident_f[:]
@@ -193,35 +190,42 @@ def tile_share_lstm_cell_pa_kernel(
         acts_t_of = {}
 
         def prepare_rows(r):
-            bank = ps_t.tile([P, 4, KT, P], BF16, name="bank_a", tag="bank_t")
+            bank = psum.tile([P, 4, KT, P], BF16, name="bank_a", tag="bank")
             for s in range(4):
                 for kt in range(KT):
                     nc.tensor.transpose(
                         bank[:, s, kt, :], acts_sb[:, s, r, kt * P : (kt + 1) * P], ident_bf[:]
                     )
-            acts_t_of[r] = stage.tile([P, 4, KT, P], BF16, name="acts_t", bufs=PREP_AHEAD + 1)
+            acts_t_of[r] = stage.tile([P, 4, KT, P], BF16, name="acts_t", bufs=2 * PAIR)
             nc.scalar.copy(out=acts_t_of[r][:], in_=bank[:])
-            x_grouped_of[r] = stage.tile(
-                [P, PASSES, P, 4], BF16, align_bytes=64, name="x_grouped", bufs=PREP_AHEAD
-            )
-            regroup(0, x_sb[:, r, :], x_grouped_of[r][:].bitcast(F32))
+            q, i = divmod(r, PAIR)
+            if i == 0:
+                x_grouped_of[q] = stage.tile(
+                    [P, PAIR, PASSES, P, 4], BF16, align_bytes=64, name="x_grouped"
+                )
+            regroup(0, x_sb[:, r, :], x_grouped_of[q][:].bitcast(F32)[:, i, :, :, :])
 
-        def quantise_x(r):
+        def rows_of(q):
+            return slice(q * PAIR, (q + 1) * PAIR)
+
+        def quantise_x(q):
             nc.vector.quantize_mx(
-                out=x_codes[:, r, :, :].rearrange("p g b -> p (g b)").bitcast(FP8X4),
-                scales=x_scales[:, r, :, :].rearrange("p g b -> p (g b)"),
-                in_=x_grouped_of[r][:].rearrange("p g b t -> p (g b t)"),
+                out=x_codes[:, rows_of(q), :, :].rearrange("p r g b -> p (r g b)").bitcast(FP8X4),
+                scales=x_scales[:, rows_of(q), :, :].rearrange("p r g b -> p (r g b)"),
+                in_=x_grouped_of[q][:].rearrange("p r g b t -> p (r g b t)"),
             )
 
         gates_of = {}
 
         def plain_rows(r):
-            gates = gate_pool.tile([P, GATES], F32, name="gates")
-            gates_of[r] = gates
+            q, i = divmod(r, PAIR)
+            if i == 0:
+                gates_of[q] = gate_pool.tile([P, PAIR, GATES], F32, name="gates")
+            gates = gates_of[q][:, i, :]
             acts_t = acts_t_of[r]
             for c0, n in CHUNKS:
                 bias_in_psum = c0 >= BIAS_IN_PSUM_FROM
-                acc = ps_acc.tile([P, BANK], F32, name="acc_plain", tag="acc")
+                acc = psum.tile([P, BANK], F32, name="acc_plain", tag="bank")
                 for g0, width, s in PLAIN_GROUPS:
                     if c0 <= g0 < c0 + n:
                         cols = acc[:, g0 - c0 : g0 - c0 + width]
@@ -245,10 +249,10 @@ def tile_share_lstm_cell_pa_kernel(
                     )
 
         def mx_rows(r, chunk_ids):
-            gates = gates_of[r]
+            gates = gates_of[r // PAIR][:, r % PAIR, :]
             for j in chunk_ids:
                 c0, n = CHUNKS[j]
-                acc = ps_acc.tile([P, BANK], F32, name="acc_mx", tag="acc")
+                acc = psum.tile([P, BANK], F32, name="acc_mx", tag="bank")
                 for g in range(PASSES):
                     nc.tensor.matmul_mx(
                         out=acc[:, 0:n],
@@ -263,123 +267,117 @@ def tile_share_lstm_cell_pa_kernel(
                     out=gates[:, c0 : c0 + n], in0=acc[:, 0:n], in1=gates[:, c0 : c0 + n], op=ALU.add
                 )
 
-        def squash(r, lo, hi, func):
-            gates = gates_of[r]
-            nc.scalar.activation(out=gates[:, lo:hi], in_=gates[:, lo:hi], func=func)
+        def squash(q, lo, hi, func):
+            gates = gates_of[q]
+            nc.scalar.activation(out=gates[:, :, lo:hi], in_=gates[:, :, lo:hi], func=func)
 
-        def squash_core(r):
-            squash(r, 0, 3 * DH, ACT.Sigmoid)
-            squash(r, 3 * DH, 4 * DH, ACT.Tanh)
+        def squash_core(q):
+            squash(q, 0, 3 * DH, ACT.Sigmoid)
+            squash(q, 3 * DH, 4 * DH, ACT.Tanh)
 
-        def squash_shared(r):
-            squash(r, 4 * DH, 7 * DH, ACT.Sigmoid)
+        def squash_shared(q):
+            squash(q, 4 * DH, 7 * DH, ACT.Sigmoid)
 
         cell_of = {}
         outs_of = {}
         t_cell_of = {}
 
-        def gate_views(r):
-            gates = gates_of[r]
-            i_g, f_g, o_g, c_hat = [gates[:, k * DH : (k + 1) * DH] for k in range(4)]
-            b_all = gates[:, 4 * DH : 7 * DH].rearrange("p (j d) -> p j d", j=3)
+        def gate_views(q):
+            gates = gates_of[q]
+            i_g, f_g, o_g, c_hat = [gates[:, :, k * DH : (k + 1) * DH] for k in range(4)]
+            b_all = gates[:, :, 4 * DH : 7 * DH].rearrange("p i (j d) -> p i j d", j=3)
             return i_g, f_g, o_g, c_hat, b_all
 
-        def combine_core(r, engine):
-            i_g, f_g, o_g, c_hat, b_all = gate_views(r)
-            cell = work.tile([P, DH], F32, name="cell")
-            fresh = work.tile([P, DH], F32, name="fresh")
-            cell_of[r] = cell
-            engine.tensor_tensor(out=cell[:], in0=f_g, in1=c_sb[:, r, :], op=ALU.mult)
+        def combine_core(q, engine):
+            i_g, f_g, o_g, c_hat, b_all = gate_views(q)
+            cell = work.tile([P, PAIR, DH], F32, name="cell")
+            fresh = work.tile([P, PAIR, DH], F32, name="fresh")
+            cell_of[q] = cell
+            engine.tensor_tensor(out=cell[:], in0=f_g, in1=c_sb[:, rows_of(q), :], op=ALU.mult)
             engine.tensor_tensor(out=fresh[:], in0=i_g, in1=c_hat, op=ALU.mult)
             engine.tensor_tensor(out=cell[:], in0=cell[:], in1=fresh[:], op=ALU.add)
 
-        def combine_shared(r, engine):
-            i_g, f_g, o_g, c_hat, b_all = gate_views(r)
+        def combine_shared(q, engine):
+            i_g, f_g, o_g, c_hat, b_all = gate_views(q)
             engine.tensor_tensor(
-                out=b_all, in0=b_all, in1=o_g.unsqueeze(1).to_broadcast([P, 3, DH]), op=ALU.subtract
+                out=b_all, in0=b_all, in1=o_g.unsqueeze(2).to_broadcast([P, PAIR, 3, DH]), op=ALU.subtract
             )
 
-        def mask_cell(r):
-            cell = cell_of[r]
-            outs = work.tile([P, 5, DH], F32, name="outs")
-            t_cell = work.tile([P, DH], F32, name="t_cell")
-            outs_of[r] = outs
-            t_cell_of[r] = t_cell
-            m = mask_f[:, r : r + 1]
-            nc.scalar.activation(out=t_cell[:], in_=cell[:], func=ACT.Tanh, scale=m)
-            nc.scalar.activation(out=t_cell[:], in_=t_cell[:], func=ACT.Copy, scale=m)
-            nc.scalar.activation(out=outs[:, 1, :], in_=cell[:], func=ACT.Copy, scale=m)
-            nc.sync.dma_start(out=out_views[1][:, r, :], in_=outs[:, 1, :])
+        def mask_cell(q):
+            cell = cell_of[q]
+            outs = work.tile([P, 5, PAIR, DH], F32, name="outs")
+            t_cell = work.tile([P, PAIR, DH], F32, name="t_cell")
+            outs_of[q] = outs
+            t_cell_of[q] = t_cell
+            row_mask = [mask_f[:, q * PAIR + i : q * PAIR + i + 1] for i in range(PAIR)]
+            for i in range(PAIR):
+                nc.scalar.activation(out=t_cell[:, i, :], in_=cell[:, i, :], func=ACT.Tanh, scale=row_mask[i])
+            for i in range(PAIR):
+                nc.scalar.activation(out=t_cell[:, i, :], in_=t_cell[:, i, :], func=ACT.Copy, scale=row_mask[i])
+            for i in range(PAIR):
+                nc.scalar.activation(out=outs[:, 1, i, :], in_=cell[:, i, :], func=ACT.Copy, scale=row_mask[i])
+            nc.sync.dma_start(out=out_views[1][:, rows_of(q), :], in_=outs[:, 1, :, :])
 
-        def finish(r):
-            i_g, f_g, o_g, c_hat, b_minus_o = gate_views(r)
-            outs = outs_of[r]
-            t_cell = t_cell_of[r]
-            h_out, c_out, s0_out, s1_out, s2_out = [outs[:, k, :] for k in range(5)]
-            e1 = work.tile([P, DH], F32, name="e1")
-            e2 = work.tile([P, DH], F32, name="e2")
+        def finish(q):
+            i_g, f_g, o_g, c_hat, b_minus_o = gate_views(q)
+            outs = outs_of[q]
+            t_cell = t_cell_of[q]
+            h_out, c_out, s0_out, s1_out, s2_out = [outs[:, k, :, :] for k in range(5)]
+            e1 = work.tile([P, PAIR, DH], F32, name="e1")
+            e2 = work.tile([P, PAIR, DH], F32, name="e2")
             stt = nc.vector.scalar_tensor_tensor
-            stt(out=s0_out, in0=b_minus_o[:, 0, :], scalar=1.0, in1=t_cell[:], op0=ALU.add, op1=ALU.mult)
+            stt(out=s0_out, in0=b_minus_o[:, :, 0, :], scalar=1.0, in1=t_cell[:], op0=ALU.add, op1=ALU.mult)
             nc.vector.tensor_tensor(out=h_out, in0=o_g, in1=t_cell[:], op=ALU.mult)
-            stt(out=e1[:], in0=b_minus_o[:, 1, :], scalar=2.0, in1=s0_out, op0=ALU.add, op1=ALU.subtract)
-            stt(out=e2[:], in0=s0_out, scalar=-2.0, in1=b_minus_o[:, 2, :], op0=ALU.mult, op1=ALU.add)
+            stt(out=e1[:], in0=b_minus_o[:, :, 1, :], scalar=2.0, in1=s0_out, op0=ALU.add, op1=ALU.subtract)
+            stt(out=e2[:], in0=s0_out, scalar=-2.0, in1=b_minus_o[:, :, 2, :], op0=ALU.mult, op1=ALU.add)
             stt(out=s1_out, in0=e1[:], scalar=0.5, in1=t_cell[:], op0=ALU.mult, op1=ALU.mult)
             stt(out=e2[:], in0=e2[:], scalar=3.0, in1=s1_out, op0=ALU.add, op1=ALU.subtract)
             stt(out=s2_out, in0=e2[:], scalar=1.0 / 3.0, in1=t_cell[:], op0=ALU.mult, op1=ALU.mult)
             for k in (0, 2, 3, 4):
-                nc.sync.dma_start(out=out_views[k][:, r, :], in_=outs[:, k, :])
+                nc.sync.dma_start(out=out_views[k][:, rows_of(q), :], in_=outs[:, k, :, :])
 
-        def helper(r):
-            return nc.vector if r >= ROW_TILES - 1 else nc.gpsimd
+        def helper(q):
+            return nc.vector if q == N_PAIRS - 1 else nc.gpsimd
 
-        def core(r):
-            mx_rows(r, CORE)
-            squash_core(r)
+        def both(stage_of_row_tile, q, *more):
+            for r in range(q * PAIR, (q + 1) * PAIR):
+                stage_of_row_tile(r, *more)
 
         transpose_plain_weights()
         broadcast_bias()
-        prepare_rows(0)
-        prepare_rows(1)
-        plain_rows(0)
+        both(prepare_rows, 0)
+        both(plain_rows, 0)
         quantise_x(0)
         regroup_weight_chunk(0)
-        quantise_x(1)
-        plain_rows(1)
         regroup_weight_chunk(1)
         quantise_weight_chunk(0)
         quantise_weight_chunk(1)
         regroup_weight_chunk(2)
-        mx_rows(0, CORE)
-        mx_rows(1, CORE)
+        both(mx_rows, 0, CORE)
         regroup_weight_chunk(3)
+        both(prepare_rows, 1)
         squash_core(0)
-        combine_core(0, helper(0))
-        squash_core(1)
-        combine_core(1, helper(1))
         quantise_weight_chunk(2)
         quantise_weight_chunk(3)
+        combine_core(0, helper(0))
         nc.vector.tensor_copy(out=mask_f[:], in_=mask_bf[:])
-        prepare_rows(2)
-        prepare_rows(3)
-        plain_rows(2)
-        prepare_rows(4)
-        quantise_x(2)
-        for n in range(-SHARED_AHEAD, ROW_TILES):
-            if n + SHARED_AHEAD < ROW_TILES:
-                mx_rows(n + SHARED_AHEAD, SHARED)
-                squash_shared(n + SHARED_AHEAD)
-                mask_cell(n + SHARED_AHEAD)
-            if PLAIN_AHEAD <= n + PLAIN_AHEAD < ROW_TILES:
-                plain_rows(n + PLAIN_AHEAD)
-            if CORE_AHEAD <= n + CORE_AHEAD < ROW_TILES:
-                core(n + CORE_AHEAD)
-            if PREP_AHEAD <= n + PREP_AHEAD < ROW_TILES:
-                prepare_rows(n + PREP_AHEAD)
-            if n + SHARED_AHEAD < ROW_TILES:
-                combine_shared(n + SHARED_AHEAD, helper(n + PLAIN_AHEAD))
-            if PLAIN_AHEAD <= n + PLAIN_AHEAD < ROW_TILES:
-                quantise_x(n + PLAIN_AHEAD)
-            if n >= 0:
-                finish(n)
-            if CORE_AHEAD <= n + CORE_AHEAD < ROW_TILES:
-                combine_core(n + CORE_AHEAD, helper(n + CORE_AHEAD))
+        quantise_x(1)
+        for q in range(N_PAIRS):
+            both(mx_rows, q, SHARED)
+            squash_shared(q)
+            if q + 1 < N_PAIRS:
+                plain_rows((q + 1) * PAIR)
+            mask_cell(q)
+            if q + 1 < N_PAIRS:
+                plain_rows((q + 1) * PAIR + 1)
+                both(mx_rows, q + 1, CORE)
+            if q + 2 < N_PAIRS:
+                both(prepare_rows, q + 2)
+            if q + 1 < N_PAIRS:
+                squash_core(q + 1)
+            combine_shared(q, helper(q))
+            finish(q)
+            if q + 2 < N_PAIRS:
+                quantise_x(q + 2)
+            if q + 1 < N_PAIRS:
+                combine_core(q + 1, helper(q + 1))

@@ -363,7 +363,8 @@ def tile_share_lstm_cell_pa_kernel(
         nc.vector.tensor_copy(out=mask_f[:], in_=mask_bf[:])
         quantise_x(1)
         for q in range(N_PAIRS):
-            both(mx_rows, q, SHARED)
+            if q + 1 < N_PAIRS or N_PAIRS == 1:
+                both(mx_rows, q, SHARED)
             squash_shared(q)
             if q + 1 < N_PAIRS:
                 plain_rows((q + 1) * PAIR)
@@ -373,6 +374,8 @@ def tile_share_lstm_cell_pa_kernel(
                 both(mx_rows, q + 1, CORE)
             if q + 2 < N_PAIRS:
                 both(prepare_rows, q + 2)
+            if q + 2 == N_PAIRS:
+                both(mx_rows, q + 1, SHARED)
             if q + 1 < N_PAIRS:
                 squash_core(q + 1)
             combine_shared(q, helper(q))

@@ -27,6 +27,7 @@ BIAS_IN_PSUM_FROM = 4 * DH
 PLAIN_ROW_TILES = GATES // P
 CORE = (0, 1)
 SHARED = (2, 3)
+PER_BANK = 4
 PAIR = 2
 N_PAIRS = ROW_TILES // PAIR
 
@@ -134,10 +135,10 @@ def tile_share_lstm_cell_pa_kernel(
 
         def transpose_plain_weights():
             turn = 0
-            for t0 in range(0, PLAIN_ROW_TILES, 8):
-                count = min(8, PLAIN_ROW_TILES - t0)
+            for t0 in range(0, PLAIN_ROW_TILES, PER_BANK):
+                count = min(PER_BANK, PLAIN_ROW_TILES - t0)
                 for kt in range(KT):
-                    bank = psum.tile([P, 8, P], BF16, name="bank_w", tag="bank")
+                    bank = psum.tile([P, PER_BANK, P], BF16, name="bank_w", tag="bank")
                     for t in range(count):
                         nc.tensor.transpose(
                             bank[:, t, :], wplain_sb[:, t0 + t, kt * P : (kt + 1) * P], ident_bf[:]
@@ -190,14 +191,15 @@ def tile_share_lstm_cell_pa_kernel(
         acts_t_of = {}
 
         def prepare_rows(r):
-            bank = psum.tile([P, 4, KT, P], BF16, name="bank_a", tag="bank")
-            for s in range(4):
-                for kt in range(KT):
-                    nc.tensor.transpose(
-                        bank[:, s, kt, :], acts_sb[:, s, r, kt * P : (kt + 1) * P], ident_bf[:]
-                    )
             acts_t_of[r] = stage.tile([P, 4, KT, P], BF16, name="acts_t", bufs=2 * PAIR)
-            nc.scalar.copy(out=acts_t_of[r][:], in_=bank[:])
+            for first in range(0, 4, PER_BANK // KT):
+                bank = psum.tile([P, PER_BANK // KT, KT, P], BF16, name="bank_a", tag="bank")
+                for s in range(PER_BANK // KT):
+                    for kt in range(KT):
+                        nc.tensor.transpose(
+                            bank[:, s, kt, :], acts_sb[:, first + s, r, kt * P : (kt + 1) * P], ident_bf[:]
+                        )
+                nc.scalar.copy(out=acts_t_of[r][:, first : first + PER_BANK // KT, :, :], in_=bank[:])
             q, i = divmod(r, PAIR)
             if i == 0:
                 x_grouped_of[q] = stage.tile(
@@ -322,14 +324,14 @@ def tile_share_lstm_cell_pa_kernel(
             i_g, f_g, o_g, c_hat, b_minus_o = gate_views(q)
             outs = outs_of[q]
             t_cell = t_cell_of[q]
-            h_out, c_out, s0_out, s1_out, s2_out = [outs[:, k, :, :] for k in range(5)]
+            h_out, c_out, firstout, s1_out, s2_out = [outs[:, k, :, :] for k in range(5)]
             e1 = work.tile([P, PAIR, DH], F32, name="e1")
             e2 = work.tile([P, PAIR, DH], F32, name="e2")
             stt = nc.vector.scalar_tensor_tensor
-            stt(out=s0_out, in0=b_minus_o[:, :, 0, :], scalar=1.0, in1=t_cell[:], op0=ALU.add, op1=ALU.mult)
+            stt(out=firstout, in0=b_minus_o[:, :, 0, :], scalar=1.0, in1=t_cell[:], op0=ALU.add, op1=ALU.mult)
             nc.vector.tensor_tensor(out=h_out, in0=o_g, in1=t_cell[:], op=ALU.mult)
-            stt(out=e1[:], in0=b_minus_o[:, :, 1, :], scalar=2.0, in1=s0_out, op0=ALU.add, op1=ALU.subtract)
-            stt(out=e2[:], in0=s0_out, scalar=-2.0, in1=b_minus_o[:, :, 2, :], op0=ALU.mult, op1=ALU.add)
+            stt(out=e1[:], in0=b_minus_o[:, :, 1, :], scalar=2.0, in1=firstout, op0=ALU.add, op1=ALU.subtract)
+            stt(out=e2[:], in0=firstout, scalar=-2.0, in1=b_minus_o[:, :, 2, :], op0=ALU.mult, op1=ALU.add)
             stt(out=s1_out, in0=e1[:], scalar=0.5, in1=t_cell[:], op0=ALU.mult, op1=ALU.mult)
             stt(out=e2[:], in0=e2[:], scalar=3.0, in1=s1_out, op0=ALU.add, op1=ALU.subtract)
             stt(out=s2_out, in0=e2[:], scalar=1.0 / 3.0, in1=t_cell[:], op0=ALU.mult, op1=ALU.mult)

from contextlib import ExitStack

import concourse.mybir as mybir
from concourse.masks import make_identity

F32 = mybir.dt.float32
BF16 = mybir.dt.bfloat16
U32 = mybir.dt.uint32
U8 = mybir.dt.uint8
FP8X4 = mybir.dt.float8_e4m3fn_x4
ACT = mybir.ActivationFunctionType
ALU = mybir.AluOpType

P = 128
BATCH = 1024
DI = 1024
DH = 256
GATES = 7 * DH
ROW_TILES = BATCH // P
K_PASS = 4 * P
PASSES = DI // K_PASS
KT = DH // P
BANK = 512
CHUNKS = ((0, 512), (512, 512), (1024, 512), (1536, 256))
PLAIN_GROUPS = ((0, 512, 0), (512, 512, 0), (1024, 256, 1), (1280, 256, 2), (1536, 256, 3))
BIAS_IN_PSUM_FROM = 4 * DH
PLAIN_ROW_TILES = GATES // P
CORE = (0, 1)
SHARED = (2, 3)
PER_BANK = 4
PAIR = 2
N_PAIRS = ROW_TILES // PAIR

FLOPS = 2 * BATCH * (GATES * DI + 4 * DH * DH + 3 * DH * DH)


def tile_share_lstm_cell_pa_kernel(
    tc, x, h_minors, c_minors, s0, s1, s2, mask,
    weight_ih, bias_ih, weight_hh, bias_hh,
    weight_sh0, bias_sh0, weight_sh1, bias_sh1, weight_sh2, bias_sh2,
    out_0, out_1, out_2, out_3, out_4,
):
    nc = tc.nc
    with ExitStack() as ctx:
        keep = ctx.enter_context(tc.tile_pool(name="keep", bufs=1))
        stage = ctx.enter_context(tc.tile_pool(name="stage", bufs=2))
        gate_pool = ctx.enter_context(tc.tile_pool(name="gate_pool", bufs=3))
        work = ctx.enter_context(tc.tile_pool(name="work", bufs=2))
        psum = ctx.enter_context(tc.psum_pool(name="psum", bufs=8))
        ctx.enter_context(tc.manual_schedule())

        def by_row_tile(ap):
            return ap.rearrange("(p r) d -> p r d", r=ROW_TILES)

        x_view = by_row_tile(x)
        act_views = [by_row_tile(a) for a in (h_minors, s0, s1, s2)]
        out_views = [by_row_tile(o) for o in (out_0, out_1, out_2, out_3, out_4)]

        x_sb = keep.tile([P, ROW_TILES, DI], BF16)
        acts_sb = keep.tile([P, 4, ROW_TILES, DH], BF16)
        c_sb = keep.tile([P, ROW_TILES, DH], BF16)
        wih_sb = keep.tile([P, GATES // P, DI], BF16)
        wplain_sb = keep.tile([P, PLAIN_ROW_TILES, DH], BF16)
        wplain_t = keep.tile([P, KT, GATES], BF16)
        bias_rows = keep.tile([P, GATES], BF16)
        bias_bc = keep.tile([P, BIAS_IN_PSUM_FROM], F32)
        mask_bf = keep.tile([P, ROW_TILES], BF16)
        mask_f = keep.tile([P, ROW_TILES], F32)
        ident_bf = keep.tile([P, P], BF16)
        ident_f = keep.tile([P, P], F32)
        ones = keep.tile([P, P], BF16)
        warm = keep.tile([P, 1], F32)
        x_codes = keep.tile([P, ROW_TILES, PASSES, P], U32, align_bytes=64)
        x_scales = keep.tile([P, ROW_TILES, PASSES, P], U8, align_bytes=64)
        w_codes = [
            keep.tile([P, PASSES, n], U32, align_bytes=64, name="w_codes%d" % j)
            for j, (c0, n) in enumerate(CHUNKS)
        ]
        w_scales = [
            keep.tile([P, PASSES, n], U8, align_bytes=64, name="w_scales%d" % j)
            for j, (c0, n) in enumerate(CHUNKS)
        ]

        nc.vector.memset(warm[:], 0.0)
        nc.vector.memset(bias_rows[:], 0.0)
        nc.vector.memset(ones[:], 1.0)
        make_identity(nc, ident_bf[:])

        def as_row(vec):
            return vec.rearrange("(o n) -> o n", o=1)

        nc.scalar.dma_start(out=bias_rows[0:1, :], in_=as_row(bias_ih))
        nc.scalar.dma_start(out=bias_rows[1:2, 0 : 4 * DH], in_=as_row(bias_hh))
        for j, b in enumerate((bias_sh0, bias_sh1, bias_sh2)):
            nc.gpsimd.dma_start(out=bias_rows[1:2, (4 + j) * DH : (5 + j) * DH], in_=as_row(b))
        nc.gpsimd.dma_start(out=mask_bf[:], in_=mask.rearrange("(p r) -> p r", r=ROW_TILES))
        make_identity(nc, ident_f[:])
        nc.scalar.activation(out=warm[:], in_=warm[:], func=ACT.Sigmoid)

        def load_weight_chunk(j):
            c0, n = CHUNKS[j]
            nc.sync.dma_start(
                out=wih_sb[:, c0 // P : (c0 + n) // P, :],
                in_=weight_ih[c0 : c0 + n, :].rearrange("(t p) k -> p t k", p=P),
            )

        def load_rows(first, count):
            rows = slice(first, first + count)
            for s in range(4):
                nc.sync.dma_start(out=acts_sb[:, s, rows, :], in_=act_views[s][:, rows, :])
            nc.sync.dma_start(out=x_sb[:, rows, :], in_=x_view[:, rows, :])

        nc.sync.dma_start(
            out=wplain_sb[:, 0:8, :], in_=weight_hh.rearrange("(t p) k -> p t k", p=P)
        )
        for j, w in enumerate((weight_sh0, weight_sh1, weight_sh2)):
            nc.sync.dma_start(
                out=wplain_sb[:, 8 + 2 * j : 10 + 2 * j, :],
                in_=w.rearrange("(t p) k -> p t k", p=P),
            )
        load_rows(0, 2)
        load_weight_chunk(0)
        load_weight_chunk(1)
        nc.sync.dma_start(out=c_sb[:], in_=by_row_tile(c_minors))
        load_weight_chunk(2)
        load_weight_chunk(3)
        load_rows(2, 2)
        load_rows(4, 4)

        def copy_out(turn, out, in_):
            if turn % 2 == 0:
                nc.scalar.copy(out=out, in_=in_)
            else:
                nc.vector.tensor_copy(out=out, in_=in_)

        def transpose_plain_weights():
            turn = 0
            for t0 in range(0, PLAIN_ROW_TILES, PER_BANK):
                count = min(PER_BANK, PLAIN_ROW_TILES - t0)
                for kt in range(KT):
                    bank = psum.tile([P, PER_BANK, P], BF16, name="bank_w", tag="bank")
                    for t in range(count):
                        nc.tensor.transpose(
                            bank[:, t, :], wplain_sb[:, t0 + t, kt * P : (kt + 1) * P], ident_bf[:]
                        )
                    copy_out(
                        turn,
                        wplain_t[:, kt, t0 * P : (t0 + count) * P],
                        bank[:, 0:count, :].rearrange("p t n -> p (t n)"),
                    )
                    turn += 1

        def broadcast_bias():
            for c0, n in CHUNKS:
                if c0 < BIAS_IN_PSUM_FROM:
                    acc = psum.tile([P, BANK], F32, name="acc_bias", tag="bank")
                    nc.tensor.matmul(
                        acc[:, 0:n], lhsT=ones[:], rhs=bias_rows[:, c0 : c0 + n], start=True, stop=True
                    )
                    nc.vector.tensor_copy(out=bias_bc[:, c0 : c0 + n], in_=acc[:, 0:n])

        def regroup(turn, rows_bf16, grouped_words):
            words = rows_bf16.bitcast(F32)
            bank = psum.tile([P, 2 * PASSES, P], F32, name="bank_q", tag="bank")
            for plane in range(2 * PASSES):
                nc.tensor.transpose(
                    bank[:, plane, :], words[:, plane * P : (plane + 1) * P], ident_f[:]
                )
            copy_out(turn, grouped_words, bank[:].rearrange("p (g u) n -> p g n u", u=2))

        w_grouped_of = {}

        def regroup_weight_chunk(j):
            c0, n = CHUNKS[j]
            grouped = stage.tile(
                [P, PASSES, n, 4], BF16, align_bytes=64, name="w_grouped", tag="w_grouped"
            )
            w_grouped_of[j] = grouped
            grouped_words = grouped[:].bitcast(F32)
            for t in range(n // P):
                regroup(t, wih_sb[:, c0 // P + t, :], grouped_words[:, :, t * P : (t + 1) * P, :])

        def quantise_weight_chunk(j):
            nc.vector.quantize_mx(
                out=w_codes[j][:].rearrange("p g n -> p (g n)").bitcast(FP8X4),
                scales=w_scales[j][:].rearrange("p g n -> p (g n)"),
                in_=w_grouped_of[j][:].rearrange("p g n t -> p (g n t)"),
            )

        x_grouped_of = {}
        acts_t_of = {}

        def prepare_rows(r):
            acts_t_of[r] = stage.tile([P, 4, KT, P], BF16, name="acts_t", bufs=2 * PAIR)
            for first in range(0, 4, PER_BANK // KT):
                bank = psum.tile([P, PER_BANK // KT, KT, P], BF16, name="bank_a", tag="bank")
                for s in range(PER_BANK // KT):
                    for kt in range(KT):
                        nc.tensor.transpose(
                            bank[:, s, kt, :], acts_sb[:, first + s, r, kt * P : (kt + 1) * P], ident_bf[:]
                        )
                nc.scalar.copy(out=acts_t_of[r][:, first : first + PER_BANK // KT, :, :], in_=bank[:])
            q, i = divmod(r, PAIR)
            if i == 0:
                x_grouped_of[q] = stage.tile(
                    [P, PAIR, PASSES, P, 4], BF16, align_bytes=64, name="x_grouped"
                )
            regroup(0, x_sb[:, r, :], x_grouped_of[q][:].bitcast(F32)[:, i, :, :, :])

        def rows_of(q):
            return slice(q * PAIR, (q + 1) * PAIR)

        def quantise_x(q):
            nc.vector.quantize_mx(
                out=x_codes[:, rows_of(q), :, :].rearrange("p r g b -> p (r g b)").bitcast(FP8X4),
                scales=x_scales[:, rows_of(q), :, :].rearrange("p r g b -> p (r g b)"),
                in_=x_grouped_of[q][:].rearrange("p r g b t -> p (r g b t)"),
            )

        gates_of = {}

        def plain_rows(r):
            q, i = divmod(r, PAIR)
            if i == 0:
                gates_of[q] = gate_pool.tile([P, PAIR, GATES], F32, name="gates")
            gates = gates_of[q][:, i, :]
            acts_t = acts_t_of[r]
            for c0, n in CHUNKS:
                bias_in_psum = c0 >= BIAS_IN_PSUM_FROM
                acc = psum.tile([P, BANK], F32, name="acc_plain", tag="bank")
                for g0, width, s in PLAIN_GROUPS:
                    if c0 <= g0 < c0 + n:
                        cols = acc[:, g0 - c0 : g0 - c0 + width]
                        for kt in range(KT):
                            nc.tensor.matmul(
                                cols,
                                lhsT=acts_t[:, s, kt, :],
                                rhs=wplain_t[:, kt, g0 : g0 + width],
                                start=(kt == 0),
                                stop=(kt == KT - 1 and not bias_in_psum),
                            )
                        if bias_in_psum:
                            nc.tensor.matmul(
                                cols, lhsT=ones[:], rhs=bias_rows[:, g0 : g0 + width], start=False, stop=True
                            )
                if bias_in_psum:
                    nc.scalar.copy(out=gates[:, c0 : c0 + n], in_=acc[:, 0:n])
                else:
                    nc.vector.tensor_tensor(
                        out=gates[:, c0 : c0 + n], in0=acc[:, 0:n], in1=bias_bc[:, c0 : c0 + n], op=ALU.add
                    )

        def mx_rows(r, chunk_ids):
            gates = gates_of[r // PAIR][:, r % PAIR, :]
            for j in chunk_ids:
                c0, n = CHUNKS[j]
                acc = psum.tile([P, BANK], F32, name="acc_mx", tag="bank")
                for g in range(PASSES):
                    nc.tensor.matmul_mx(
                        out=acc[:, 0:n],
                        lhsT=x_codes[:, r, g, :].bitcast(FP8X4),
                        lhsT_scale=x_scales[:, r, g, :],
                        rhs=w_codes[j][:, g, :].bitcast(FP8X4),
                        rhs_scale=w_scales[j][:, g, :],
                        start=(g == 0),
                        stop=(g == PASSES - 1),
                    )
                nc.vector.tensor_tensor(
                    out=gates[:, c0 : c0 + n], in0=acc[:, 0:n], in1=gates[:, c0 : c0 + n], op=ALU.add
                )

        def squash(q, lo, hi, func):
            gates = gates_of[q]
            nc.scalar.activation(out=gates[:, :, lo:hi], in_=gates[:, :, lo:hi], func=func)

        def squash_core(q):
            squash(q, 0, 3 * DH, ACT.Sigmoid)
            squash(q, 3 * DH, 4 * DH, ACT.Tanh)

        def squash_shared(q):
            squash(q, 4 * DH, 7 * DH, ACT.Sigmoid)

        cell_of = {}
        outs_of = {}
        t_cell_of = {}

        def gate_views(q):
            gates = gates_of[q]
            i_g, f_g, o_g, c_hat = [gates[:, :, k * DH : (k + 1) * DH] for k in range(4)]
            b_all = gates[:, :, 4 * DH : 7 * DH].rearrange("p i (j d) -> p i j d", j=3)
            return i_g, f_g, o_g, c_hat, b_all

        def combine_core(q, engine):
            i_g, f_g, o_g, c_hat, b_all = gate_views(q)
            cell = work.tile([P, PAIR, DH], F32, name="cell")
            fresh = work.tile([P, PAIR, DH], F32, name="fresh")
            cell_of[q] = cell
            engine.tensor_tensor(out=cell[:], in0=f_g, in1=c_sb[:, rows_of(q), :], op=ALU.mult)
            engine.tensor_tensor(out=fresh[:], in0=i_g, in1=c_hat, op=ALU.mult)
            engine.tensor_tensor(out=cell[:], in0=cell[:], in1=fresh[:], op=ALU.add)

        def combine_shared(q, engine):
            i_g, f_g, o_g, c_hat, b_all = gate_views(q)
            engine.tensor_tensor(
                out=b_all, in0=b_all, in1=o_g.unsqueeze(2).to_broadcast([P, PAIR, 3, DH]), op=ALU.subtract
            )

        def mask_cell(q):
            cell = cell_of[q]
            outs = work.tile([P, 5, PAIR, DH], F32, name="outs")
            t_cell = work.tile([P, PAIR, DH], F32, name="t_cell")
            outs_of[q] = outs
            t_cell_of[q] = t_cell
            row_mask = [mask_f[:, q * PAIR + i : q * PAIR + i + 1] for i in range(PAIR)]
            for i in range(PAIR):
                nc.scalar.activation(out=t_cell[:, i, :], in_=cell[:, i, :], func=ACT.Tanh, scale=row_mask[i])
            for i in range(PAIR):
                nc.scalar.activation(out=t_cell[:, i, :], in_=t_cell[:, i, :], func=ACT.Copy, scale=row_mask[i])
            for i in range(PAIR):
                nc.scalar.activation(out=outs[:, 1, i, :], in_=cell[:, i, :], func=ACT.Copy, scale=row_mask[i])
            nc.sync.dma_start(out=out_views[1][:, rows_of(q), :], in_=outs[:, 1, :, :])

        def finish(q):
            i_g, f_g, o_g, c_hat, b_minus_o = gate_views(q)
            outs = outs_of[q]
            t_cell = t_cell_of[q]
            h_out, c_out, firstout, s1_out, s2_out = [outs[:, k, :, :] for k in range(5)]
            e1 = work.tile([P, PAIR, DH], F32, name="e1")
            e2 = work.tile([P, PAIR, DH], F32, name="e2")
            stt = nc.vector.scalar_tensor_tensor
            stt(out=firstout, in0=b_minus_o[:, :, 0, :], scalar=1.0, in1=t_cell[:], op0=ALU.add, op1=ALU.mult)
            nc.vector.tensor_tensor(out=h_out, in0=o_g, in1=t_cell[:], op=ALU.mult)
            stt(out=e1[:], in0=b_minus_o[:, :, 1, :], scalar=2.0, in1=firstout, op0=ALU.add, op1=ALU.subtract)
            stt(out=e2[:], in0=firstout, scalar=-2.0, in1=b_minus_o[:, :, 2, :], op0=ALU.mult, op1=ALU.add)
            stt(out=s1_out, in0=e1[:], scalar=0.5, in1=t_cell[:], op0=ALU.mult, op1=ALU.mult)
            stt(out=e2[:], in0=e2[:], scalar=3.0, in1=s1_out, op0=ALU.add, op1=ALU.subtract)
            stt(out=s2_out, in0=e2[:], scalar=1.0 / 3.0, in1=t_cell[:], op0=ALU.mult, op1=ALU.mult)
            for k in (0, 2, 3, 4):
                nc.sync.dma_start(out=out_views[k][:, rows_of(q), :], in_=outs[:, k, :, :])

        def helper(q):
            return nc.vector if q == N_PAIRS - 1 else nc.gpsimd

        def both(stage_of_row_tile, q, *more):
            for r in range(q * PAIR, (q + 1) * PAIR):
                stage_of_row_tile(r, *more)

        transpose_plain_weights()
        broadcast_bias()
        both(prepare_rows, 0)
        both(plain_rows, 0)
        quantise_x(0)
        regroup_weight_chunk(0)
        regroup_weight_chunk(1)
        quantise_weight_chunk(0)
        quantise_weight_chunk(1)
        regroup_weight_chunk(2)
        both(mx_rows, 0, CORE)
        regroup_weight_chunk(3)
        both(prepare_rows, 1)
        squash_core(0)
        quantise_weight_chunk(2)
        quantise_weight_chunk(3)
        combine_core(0, helper(0))
        nc.vector.tensor_copy(out=mask_f[:], in_=mask_bf[:])
        quantise_x(1)
        for q in range(N_PAIRS):
            if q + 1 < N_PAIRS or N_PAIRS == 1:
                both(mx_rows, q, SHARED)
            squash_shared(q)
            if q + 1 < N_PAIRS:
                plain_rows((q + 1) * PAIR)
            mask_cell(q)
            if q + 1 < N_PAIRS:
                plain_rows((q + 1) * PAIR + 1)
                both(mx_rows, q + 1, CORE)
            if q + 2 < N_PAIRS:
                both(prepare_rows, q + 2)
            if q + 2 == N_PAIRS:
                both(mx_rows, q + 1, SHARED)
            if q + 1 < N_PAIRS:
                squash_core(q + 1)
            combine_shared(q, helper(q))
            finish(q)
            if q + 2 < N_PAIRS:
                quantise_x(q + 2)
            if q + 1 < N_PAIRS:
                combine_core(q + 1, helper(q + 1))
